import numpy as np
import ml_dtypes


def mxq(x, axis, fmt="e4m3"):
    dtype, down = {"e4m3": (ml_dtypes.float8_e4m3fn, 7), "e5m2": (ml_dtypes.float8_e5m2, 14)}[fmt]
    v = np.moveaxis(np.asarray(x, np.float32).astype(ml_dtypes.bfloat16).astype(np.float64), axis, -1)
    blocks = v.reshape(v.shape[:-1] + (-1, 32))
    amax = np.abs(blocks).max(-1, keepdims=True)
    byte = np.maximum(np.where(amax > 0, np.frexp(amax)[1] - 1 + 127, 0) - down, 1)
    scale = np.exp2(byte - 127.0)
    codes = (blocks / scale).astype(np.float32).astype(dtype).astype(np.float64)
    return np.moveaxis((codes * scale).reshape(v.shape), -1, axis)


WIDE = False


def mx_kscale(k):
    if not WIDE:
        return np.ones(k)
    levels = np.array([10, -10, 5, -5, 0])
    a = np.random.permutation(np.resize(levels, k // 512 * 4)).reshape(k // 512, 4)
    idx = np.arange(k)
    return np.exp2(a[idx // 512, idx % 128 // 32])


BF16 = ml_dtypes.bfloat16


def bf(x):
    return np.asarray(x, np.float32).astype(BF16)


def f64(x):
    return np.asarray(x).astype(np.float64)


B, C, IN, H, ND, NG, NL = 32, 128, 512, 256, 2, 4, 2
N = B * C
USED = [0, 2, 3]


def sigmoid(v):
    return 1.0 / (1.0 + np.exp(-v))


def cell(inq, w, b1, b2):
    wu = w.reshape(NG, H, -1)[USED].reshape(len(USED) * H, -1)
    gates = (inq @ mxq(wu.T, 0, "e4m3")) + b1.reshape(NG, H)[USED].reshape(-1) + b2.reshape(NG, H)[USED].reshape(-1)
    i, g, o = np.split(gates, len(USED), axis=-1)
    c = sigmoid(i) * np.tanh(g)
    return sigmoid(o) * np.tanh(c)


def setup_inputs():
    s = mx_kscale(IN)
    return {"x": bf(np.random.standard_normal((B, C, IN)) * s),
            "w_ih": bf(np.random.standard_normal((ND, NG * H, IN)) * 1.5 / np.sqrt(IN) / s),
            "b_ih": bf(np.random.standard_normal((ND, NG * H)) * 0.3),
            "b_hh": bf(np.random.standard_normal((ND, NG * H)) * 0.3)}


def reference(x, w_ih, b_ih, b_hh):
    xq = mxq(f64(x).reshape(N, IN), 1, "e4m3")
    w, b1, b2 = f64(w_ih), f64(b_ih), f64(b_hh)
    return np.concatenate([cell(xq, w[d], b1[d], b2[d]) for d in range(ND)], axis=-1)

@@ -1,0 +1,246 @@
+from contextlib import ExitStack
+
+import concourse.masks as masks
+import concourse.mybir as mybir
+
+F32 = mybir.dt.float32
+BF16 = mybir.dt.bfloat16
+U32 = mybir.dt.uint32
+U8 = mybir.dt.uint8
+FP8X4 = mybir.dt.float8_e4m3fn_x4
+ACT = mybir.ActivationFunctionType
+ALU = mybir.AluOpType
+
+P = 128
+ROWS = 4096
+K = 512
+H = 256
+ND = 2
+CHUNK = 512
+NCHUNK = ROWS // CHUNK
+RT = CHUNK // P
+NQ = 4
+GATE_I, GATE_G, GATE_O = 0, 2, 3
+PATTERN = (("o", 0), ("c", 0), ("o", 1), ("c", 1), ("o", 2), ("c", 2), ("o", 3), ("c", 3), ("x", 0), ("x", 1))
+RA, RV = 5, 3
+DEPTH = {"s_i": 2, "t_g": 2, "cell": 3, "s_o": 3, "t_c": 3, "hid": 3}
+
+FLOPS = 2 * ROWS * (3 * H * ND) * K
+BYTES = ROWS * K * 2 + ND * 3 * H * K * 2 + 2 * ND * 3 * H * 2 + ROWS * ND * H * 4
+
+
+def tile_lstmnetwork_pa_t_kernel(tc, x, w_ih, b_ih, b_hh, out):
+    nc = tc.nc
+    xv = x.flatten_outer_dims().rearrange("(c r t) k -> c r (t k)", r=P, t=RT)
+    outv = out.rearrange("(c r t) n -> c r (t n)", r=P, t=RT)
+
+    with ExitStack() as ctx:
+        ctx.enter_context(tc.manual_schedule())
+        const = ctx.enter_context(tc.tile_pool(name="const", bufs=1))
+        xin = ctx.enter_context(tc.tile_pool(name="xin", bufs=1))
+        stage = ctx.enter_context(tc.tile_pool(name="stage", bufs=2))
+        xq = ctx.enter_context(tc.tile_pool(name="xq", bufs=3))
+        work = ctx.enter_context(tc.tile_pool(name="work", bufs=2))
+        ring_a = ctx.enter_context(tc.psum_pool(name="ring_a", bufs=RA))
+        ring_v = ctx.enter_context(tc.psum_pool(name="ring_v", bufs=RV))
+
+        bi = const.tile([16, P], BF16, name="bi")
+        bh = const.tile([16, P], BF16, name="bh")
+        nc.scalar.dma_start(out=bi[:], in_=b_ih.rearrange("d (g p) -> (d g) p", p=P))
+        nc.scalar.dma_start(out=bh[:], in_=b_hh.rearrange("d (g p) -> (d g) p", p=P))
+        warm = const.tile([P, 1], F32, name="warm")
+        nc.vector.memset(warm[:], 0.0)
+        nc.scalar.activation(out=warm[:], in_=warm[:], func=ACT.Sigmoid)
+        ident = const.tile([P, P], F32, name="ident")
+        masks.make_identity(nc, ident[:])
+        bsum = const.tile([P, P], F32, name="bsum")
+        nc.vector.memset(bsum[:], 0.0)
+
+        w_raw = {}
+        x_raw = {}
+
+        def load_w(gate, d):
+            t = const.tile([P, 2 * K], BF16, name="wraw%d_%d" % (gate, d))
+            nc.sync.dma_start(
+                out=t[:].rearrange("p (h k) -> p h k", h=2),
+                in_=w_ih[d, gate * H : (gate + 1) * H, :].rearrange("(h p) k -> p h k", p=P),
+            )
+            w_raw[(gate, d)] = t
+
+        def load_x(c, pieces):
+            t = xin.tile([P, RT * K], BF16, name="xraw%d" % c)
+            step = RT * K // pieces
+            for i in range(pieces):
+                nc.sync.dma_start(out=t[:, i * step : (i + 1) * step], in_=xv[c][:, i * step : (i + 1) * step])
+            x_raw[c] = t
+
+        load_x(0, 2)
+        load_w(GATE_I, 0)
+        load_w(GATE_I, 1)
+        load_w(GATE_G, 0)
+        load_w(GATE_G, 1)
+        load_w(GATE_O, 0)
+        load_w(GATE_O, 1)
+        for c in range(1, NCHUNK):
+            load_x(c, 1)
+
+        def turn(raw, first):
+            raw32 = raw[:].bitcast(F32)
+            bank = ring_v.tile([P, 512], F32, name="turn", tag="v")
+            for j in range(2):
+                for u in range(2):
+                    nc.tensor.transpose(
+                        bank[:, (2 * j + u) * P : (2 * j + u + 1) * P],
+                        raw32[:, (first + j) * 256 + u * P : (first + j) * 256 + (u + 1) * P],
+                        ident[:],
+                    )
+            return bank
+
+        def regroup(engine_copy, bank, grouped, pair):
+            g32 = grouped[:].bitcast(F32)
+            engine_copy(
+                out=g32[:, pair * 512 : (pair + 1) * 512].rearrange("p (j r u) -> p j r u", j=2, u=2),
+                in_=bank[:].rearrange("p (j u r) -> p j r u", j=2, u=2),
+            )
+
+        w_grp = {}
+        w_codes = {}
+        w_scales = {}
+
+        def turn_w(gate, d, engine_copy):
+            grouped = stage.tile([P, 4 * 2 * P], BF16, name="wgrp", align_bytes=64, bufs=3)
+            regroup(engine_copy, turn(w_raw[(gate, d)], 0), grouped, 0)
+            w_grp[(gate, d)] = grouped
+
+        def quant_w(gate, d):
+            codes = const.tile([P, 2 * P], U32, name="wc%d_%d" % (gate, d), align_bytes=64)
+            scales = const.tile([P, 2 * P], U8, name="ws%d_%d" % (gate, d), align_bytes=64)
+            nc.vector.quantize_mx(out=codes[:].bitcast(FP8X4), scales=scales[:], in_=w_grp[(gate, d)][:])
+            w_codes[(gate, d)] = codes
+            w_scales[(gate, d)] = scales
+
+        x_grp = {}
+        x_codes = {}
+        x_scales = {}
+
+        def turn_x(c, pair):
+            if pair == 0:
+                x_grp[c] = stage.tile([P, 4 * CHUNK], BF16, name="xgrp", align_bytes=64)
+            regroup(nc.vector.tensor_copy, turn(x_raw[c], 2 * pair), x_grp[c], pair)
+
+        def quant_x(c):
+            codes = xq.tile([P, CHUNK], U32, name="xc", align_bytes=64)
+            scales = xq.tile([P, CHUNK], U8, name="xs", align_bytes=64)
+            nc.vector.quantize_mx(out=codes[:].bitcast(FP8X4), scales=scales[:], in_=x_grp[c][:])
+            x_codes[c] = codes
+            x_scales[c] = scales
+
+        bias = const.tile([P, 16], F32, name="bias")
+        tiles = {}
+
+        def buf(c, name):
+            if (c, name) not in tiles:
+                tiles[(c, name)] = work.tile([P, NQ * CHUNK], F32, name=name, bufs=DEPTH[name])
+            return tiles[(c, name)]
+
+        def gate_act(c, gate, q, func, name):
+            d, h = divmod(q, 2)
+            acc = ring_a.tile([P, CHUNK], F32, name="acc", tag="a")
+            nc.tensor.matmul_mx(
+                out=acc[:],
+                lhsT=w_codes[(gate, d)][:, h * P : (h + 1) * P].bitcast(FP8X4),
+                lhsT_scale=w_scales[(gate, d)][:, h * P : (h + 1) * P],
+                rhs=x_codes[c][:].bitcast(FP8X4),
+                rhs_scale=x_scales[c][:],
+                start=True,
+                stop=True,
+            )
+            col = d * 8 + gate * 2 + h
+            nc.scalar.activation(
+                out=buf(c, name)[:, q * CHUNK : (q + 1) * CHUNK],
+                in_=acc[:],
+                func=func,
+                bias=bias[:, col : col + 1],
+                scale=1.0,
+            )
+
+        def cell_product(c, q, engine):
+            sl = slice(q * CHUNK, (q + 1) * CHUNK)
+            engine.tensor_tensor(
+                out=buf(c, "cell")[:, sl], in0=buf(c, "s_i")[:, sl], in1=buf(c, "t_g")[:, sl], op=ALU.mult
+            )
+
+        def turn_back(pool, tag, src, t):
+            bank = pool.tile([P, 512], F32, name="back_" + tag, tag=tag)
+            for q in range(NQ):
+                nc.tensor.transpose(
+                    bank[:, q * P : (q + 1) * P], src[:, q * CHUNK + t * P : q * CHUNK + (t + 1) * P], ident[:]
+                )
+            return bank
+
+        def cell_tanh(c, t):
+            bank = turn_back(ring_a, "a", buf(c, "cell"), t)
+            nc.scalar.activation(out=buf(c, "t_c")[:, t * 512 : (t + 1) * 512], in_=bank[:], func=ACT.Tanh)
+
+        def hidden(c, t):
+            bank = turn_back(ring_v, "v", buf(c, "s_o"), t)
+            sl = slice(t * 512, (t + 1) * 512)
+            nc.vector.tensor_tensor(out=buf(c, "hid")[:, sl], in0=bank[:], in1=buf(c, "t_c")[:, sl], op=ALU.mult)
+
+        nc.vector.tensor_tensor(out=bsum[0:16, :], in0=bi[:], in1=bh[:], op=ALU.add)
+        turn_x(0, 0)
+        turn_x(0, 1)
+        turn_w(GATE_I, 0, nc.scalar.copy)
+        turn_w(GATE_I, 1, nc.scalar.copy)
+        quant_x(0)
+        quant_w(GATE_I, 0)
+        bias_ps = ring_v.tile([P, 512], F32, name="bias_ps", tag="v")
+        nc.tensor.transpose(bias_ps[:, 0:P], bsum[:], ident[:])
+        nc.vector.tensor_copy(out=bias[:], in_=bias_ps[:, 0:16])
+        quant_w(GATE_I, 1)
+        turn_w(GATE_G, 0, nc.vector.tensor_copy)
+        turn_w(GATE_G, 1, nc.vector.tensor_copy)
+        for q in range(NQ):
+            gate_act(0, GATE_I, q, ACT.Sigmoid, "s_i")
+        quant_w(GATE_G, 0)
+        quant_w(GATE_G, 1)
+        turn_w(GATE_O, 0, nc.vector.tensor_copy)
+        turn_w(GATE_O, 1, nc.vector.tensor_copy)
+        quant_w(GATE_O, 0)
+        quant_w(GATE_O, 1)
+
+        def store(c, t0, t1):
+            nc.sync.dma_start(out=outv[c][:, t0 * 512 : t1 * 512], in_=buf(c, "hid")[:, t0 * 512 : t1 * 512])
+
+        for c in range(NCHUNK):
+            last = c == NCHUNK - 1
+            if c > 0:
+                for q in range(NQ):
+                    gate_act(c, GATE_I, q, ACT.Sigmoid, "s_i")
+            for q in range(NQ):
+                gate_act(c, GATE_G, q, ACT.Tanh, "t_g")
+            for kind, t in PATTERN:
+                if kind == "c" and c >= 1:
+                    cell_tanh(c - 1, t)
+                if kind == "o" and c >= 2:
+                    hidden(c - 2, t)
+                if kind == "x" and not last:
+                    turn_x(c + 1, t)
+            if not last:
+                quant_x(c + 1)
+            if c >= 2:
+                store(c - 2, 0, RT)
+            for q in range(NQ):
+                cell_product(c, q, nc.vector if last and q >= 2 else nc.gpsimd)
+            for q in range(NQ):
+                gate_act(c, GATE_O, q, ACT.Sigmoid, "s_o")
+        c = NCHUNK - 1
+        for t in range(RT):
+            hidden(c - 1, t)
+            if t % 2 == 1:
+                store(c - 1, t - 1, t + 1)
+        for t in range(RT):
+            cell_tanh(c, t)
+        for t in range(RT):
+            hidden(c, t)
+            store(c, t, t + 1)

@@ -231,7 +231,7 @@ def tile_lstmnetwork_pa_t_kernel(tc, x, w_ih, b_ih, b_hh, out):
             if c >= 2:
                 store(c - 2, 0, RT)
             for q in range(NQ):
-                cell_product(c, q, nc.vector if last and q >= 2 else nc.gpsimd)
+                cell_product(c, q, nc.vector)
             for q in range(NQ):
                 gate_act(c, GATE_O, q, ACT.Sigmoid, "s_o")
         c = NCHUNK - 1

@@ -23,6 +23,9 @@ NQ = 4
 GATE_I, GATE_G, GATE_O = 0, 2, 3
 PATTERN = (("o", 0), ("c", 0), ("o", 1), ("c", 1), ("o", 2), ("c", 2), ("o", 3), ("c", 3), ("x", 0), ("x", 1))
 RA, RV = 5, 3
+LAST_PIECES = 1
+NWARM = 4
+TAIL = (("o", 0), ("o", 1), ("o", 2), ("c", 0), ("c", 1), ("o", 3), ("c", 2), ("c", 3))
 DEPTH = {"s_i": 2, "t_g": 2, "cell": 3, "s_o": 3, "t_c": 3, "hid": 3}
 
 FLOPS = 2 * ROWS * (3 * H * ND) * K
@@ -48,6 +51,11 @@ def tile_lstmnetwork_pa_t_kernel(tc, x, w_ih, b_ih, b_hh, out):
         bh = const.tile([16, P], BF16, name="bh")
         nc.scalar.dma_start(out=bi[:], in_=b_ih.rearrange("d (g p) -> (d g) p", p=P))
         nc.scalar.dma_start(out=bh[:], in_=b_hh.rearrange("d (g p) -> (d g) p", p=P))
+        zeros = const.tile([P, 512], BF16, name="zeros")
+        nc.vector.memset(zeros[:], 0.0)
+        spin = ring_a.tile([P, 512], F32, name="spin", tag="a")
+        for i in range(NWARM):
+            nc.tensor.matmul(out=spin[:], lhsT=zeros[:, 0:P], rhs=zeros[:], start=True, stop=True)
         warm = const.tile([P, 1], F32, name="warm")
         nc.vector.memset(warm[:], 0.0)
         nc.scalar.activation(out=warm[:], in_=warm[:], func=ACT.Sigmoid)
@@ -123,17 +131,18 @@ def tile_lstmnetwork_pa_t_kernel(tc, x, w_ih, b_ih, b_hh, out):
         x_codes = {}
         x_scales = {}
 
-        def turn_x(c, pair):
+        def turn_x(c, pair, engine_copy):
             if pair == 0:
                 x_grp[c] = stage.tile([P, 4 * CHUNK], BF16, name="xgrp", align_bytes=64)
-            regroup(nc.vector.tensor_copy, turn(x_raw[c], 2 * pair), x_grp[c], pair)
+            regroup(engine_copy, turn(x_raw[c], 2 * pair), x_grp[c], pair)
 
-        def quant_x(c):
-            codes = xq.tile([P, CHUNK], U32, name="xc", align_bytes=64)
-            scales = xq.tile([P, CHUNK], U8, name="xs", align_bytes=64)
-            nc.vector.quantize_mx(out=codes[:].bitcast(FP8X4), scales=scales[:], in_=x_grp[c][:])
-            x_codes[c] = codes
-            x_scales[c] = scales
+        def quant_x(c, lo, hi):
+            if c not in x_codes:
+                x_codes[c] = xq.tile([P, CHUNK], U32, name="xc", align_bytes=64)
+                x_scales[c] = xq.tile([P, CHUNK], U8, name="xs", align_bytes=64)
+            nc.vector.quantize_mx(
+                out=x_codes[c][:, lo:hi].bitcast(FP8X4), scales=x_scales[c][:, lo:hi], in_=x_grp[c][:, 4 * lo : 4 * hi]
+            )
 
         bias = const.tile([P, 16], F32, name="bias")
         tiles = {}
@@ -143,21 +152,21 @@ def tile_lstmnetwork_pa_t_kernel(tc, x, w_ih, b_ih, b_hh, out):
                 tiles[(c, name)] = work.tile([P, NQ * CHUNK], F32, name=name, bufs=DEPTH[name])
             return tiles[(c, name)]
 
-        def gate_act(c, gate, q, func, name):
+        def gate_act(c, gate, q, func, name, lo=0, hi=CHUNK):
             d, h = divmod(q, 2)
-            acc = ring_a.tile([P, CHUNK], F32, name="acc", tag="a")
+            acc = ring_a.tile([P, hi - lo], F32, name="acc", tag="a")
             nc.tensor.matmul_mx(
                 out=acc[:],
                 lhsT=w_codes[(gate, d)][:, h * P : (h + 1) * P].bitcast(FP8X4),
                 lhsT_scale=w_scales[(gate, d)][:, h * P : (h + 1) * P],
-                rhs=x_codes[c][:].bitcast(FP8X4),
-                rhs_scale=x_scales[c][:],
+                rhs=x_codes[c][:, lo:hi].bitcast(FP8X4),
+                rhs_scale=x_scales[c][:, lo:hi],
                 start=True,
                 stop=True,
             )
             col = d * 8 + gate * 2 + h
             nc.scalar.activation(
-                out=buf(c, name)[:, q * CHUNK : (q + 1) * CHUNK],
+                out=buf(c, name)[:, q * CHUNK + lo : q * CHUNK + hi],
                 in_=acc[:],
                 func=func,
                 bias=bias[:, col : col + 1],
@@ -178,21 +187,33 @@ def tile_lstmnetwork_pa_t_kernel(tc, x, w_ih, b_ih, b_hh, out):
                 )
             return bank
 
-        def cell_tanh(c, t):
+        def cell_tanh(c, t, pieces=1):
             bank = turn_back(ring_a, "a", buf(c, "cell"), t)
-            nc.scalar.activation(out=buf(c, "t_c")[:, t * 512 : (t + 1) * 512], in_=bank[:], func=ACT.Tanh)
+            w = 512 // pieces
+            for i in range(pieces):
+                nc.scalar.activation(
+                    out=buf(c, "t_c")[:, t * 512 + i * w : t * 512 + (i + 1) * w],
+                    in_=bank[:, i * w : (i + 1) * w],
+                    func=ACT.Tanh,
+                )
 
-        def hidden(c, t):
+        def hidden(c, t, pieces=1):
             bank = turn_back(ring_v, "v", buf(c, "s_o"), t)
-            sl = slice(t * 512, (t + 1) * 512)
-            nc.vector.tensor_tensor(out=buf(c, "hid")[:, sl], in0=bank[:], in1=buf(c, "t_c")[:, sl], op=ALU.mult)
+            w = 512 // pieces
+            for i in range(pieces):
+                sl = slice(t * 512 + i * w, t * 512 + (i + 1) * w)
+                nc.vector.tensor_tensor(
+                    out=buf(c, "hid")[:, sl], in0=bank[:, i * w : (i + 1) * w], in1=buf(c, "t_c")[:, sl], op=ALU.mult
+                )
+                if c == NCHUNK - 1 and t == RT - 1:
+                    nc.sync.dma_start(out=outv[c][:, sl], in_=buf(c, "hid")[:, sl])
 
         nc.vector.tensor_tensor(out=bsum[0:16, :], in0=bi[:], in1=bh[:], op=ALU.add)
-        turn_x(0, 0)
-        turn_x(0, 1)
+        turn_x(0, 0, nc.vector.tensor_copy)
+        turn_x(0, 1, nc.vector.tensor_copy)
         turn_w(GATE_I, 0, nc.scalar.copy)
         turn_w(GATE_I, 1, nc.scalar.copy)
-        quant_x(0)
+        quant_x(0, 0, CHUNK)
         quant_w(GATE_I, 0)
         bias_ps = ring_v.tile([P, 512], F32, name="bias_ps", tag="v")
         nc.tensor.transpose(bias_ps[:, 0:P], bsum[:], ident[:])
@@ -225,9 +246,9 @@ def tile_lstmnetwork_pa_t_kernel(tc, x, w_ih, b_ih, b_hh, out):
                 if kind == "o" and c >= 2:
                     hidden(c - 2, t)
                 if kind == "x" and not last:
-                    turn_x(c + 1, t)
+                    turn_x(c + 1, t, nc.vector.tensor_copy)
             if not last:
-                quant_x(c + 1)
+                quant_x(c + 1, 0, CHUNK)
             if c >= 2:
                 store(c - 2, 0, RT)
             for q in range(NQ):
@@ -235,12 +256,14 @@ def tile_lstmnetwork_pa_t_kernel(tc, x, w_ih, b_ih, b_hh, out):
             for q in range(NQ):
                 gate_act(c, GATE_O, q, ACT.Sigmoid, "s_o")
         c = NCHUNK - 1
-        for t in range(RT):
-            hidden(c - 1, t)
-            if t % 2 == 1:
-                store(c - 1, t - 1, t + 1)
-        for t in range(RT):
-            cell_tanh(c, t)
-        for t in range(RT):
+        for kind, t in TAIL:
+            if kind == "o":
+                hidden(c - 1, t)
+                if t % 2 == 1:
+                    store(c - 1, t - 1, t + 1)
+            else:
+                cell_tanh(c, t, LAST_PIECES if t == RT - 1 else 1)
+        for t in range(RT - 1):
             hidden(c, t)
             store(c, t, t + 1)
+        hidden(c, RT - 1, LAST_PIECES)

@@ -21,12 +21,6 @@ NCHUNK = ROWS // CHUNK
 RT = CHUNK // P
 NQ = 4
 GATE_I, GATE_G, GATE_O = 0, 2, 3
-PATTERN = (("o", 0), ("c", 0), ("o", 1), ("c", 1), ("o", 2), ("c", 2), ("o", 3), ("c", 3), ("x", 0), ("x", 1))
-RA, RV = 5, 3
-LAST_PIECES = 1
-NWARM = 4
-TAIL = (("o", 0), ("o", 1), ("o", 2), ("c", 0), ("c", 1), ("o", 3), ("c", 2), ("c", 3))
-DEPTH = {"s_i": 2, "t_g": 2, "cell": 3, "s_o": 3, "t_c": 3, "hid": 3}
 
 FLOPS = 2 * ROWS * (3 * H * ND) * K
 BYTES = ROWS * K * 2 + ND * 3 * H * K * 2 + 2 * ND * 3 * H * 2 + ROWS * ND * H * 4
@@ -44,18 +38,13 @@ def tile_lstmnetwork_pa_t_kernel(tc, x, w_ih, b_ih, b_hh, out):
         stage = ctx.enter_context(tc.tile_pool(name="stage", bufs=2))
         xq = ctx.enter_context(tc.tile_pool(name="xq", bufs=3))
         work = ctx.enter_context(tc.tile_pool(name="work", bufs=2))
-        ring_a = ctx.enter_context(tc.psum_pool(name="ring_a", bufs=RA))
-        ring_v = ctx.enter_context(tc.psum_pool(name="ring_v", bufs=RV))
+        ring_a = ctx.enter_context(tc.psum_pool(name="ring_a", bufs=5))
+        ring_v = ctx.enter_context(tc.psum_pool(name="ring_v", bufs=3))
 
         bi = const.tile([16, P], BF16, name="bi")
         bh = const.tile([16, P], BF16, name="bh")
         nc.scalar.dma_start(out=bi[:], in_=b_ih.rearrange("d (g p) -> (d g) p", p=P))
         nc.scalar.dma_start(out=bh[:], in_=b_hh.rearrange("d (g p) -> (d g) p", p=P))
-        zeros = const.tile([P, 512], BF16, name="zeros")
-        nc.vector.memset(zeros[:], 0.0)
-        spin = ring_a.tile([P, 512], F32, name="spin", tag="a")
-        for i in range(NWARM):
-            nc.tensor.matmul(out=spin[:], lhsT=zeros[:, 0:P], rhs=zeros[:], start=True, stop=True)
         warm = const.tile([P, 1], F32, name="warm")
         nc.vector.memset(warm[:], 0.0)
         nc.scalar.activation(out=warm[:], in_=warm[:], func=ACT.Sigmoid)
@@ -131,51 +120,50 @@ def tile_lstmnetwork_pa_t_kernel(tc, x, w_ih, b_ih, b_hh, out):
         x_codes = {}
         x_scales = {}
 
-        def turn_x(c, pair, engine_copy):
+        def turn_x(c, pair):
             if pair == 0:
                 x_grp[c] = stage.tile([P, 4 * CHUNK], BF16, name="xgrp", align_bytes=64)
-            regroup(engine_copy, turn(x_raw[c], 2 * pair), x_grp[c], pair)
+            regroup(nc.vector.tensor_copy, turn(x_raw[c], 2 * pair), x_grp[c], pair)
 
-        def quant_x(c, lo, hi):
-            if c not in x_codes:
-                x_codes[c] = xq.tile([P, CHUNK], U32, name="xc", align_bytes=64)
-                x_scales[c] = xq.tile([P, CHUNK], U8, name="xs", align_bytes=64)
-            nc.vector.quantize_mx(
-                out=x_codes[c][:, lo:hi].bitcast(FP8X4), scales=x_scales[c][:, lo:hi], in_=x_grp[c][:, 4 * lo : 4 * hi]
-            )
+        def quant_x(c):
+            codes = xq.tile([P, CHUNK], U32, name="xc", align_bytes=64)
+            scales = xq.tile([P, CHUNK], U8, name="xs", align_bytes=64)
+            nc.vector.quantize_mx(out=codes[:].bitcast(FP8X4), scales=scales[:], in_=x_grp[c][:])
+            x_codes[c] = codes
+            x_scales[c] = scales
 
         bias = const.tile([P, 16], F32, name="bias")
         tiles = {}
 
         def buf(c, name):
             if (c, name) not in tiles:
-                tiles[(c, name)] = work.tile([P, NQ * CHUNK], F32, name=name, bufs=DEPTH[name])
+                tiles[(c, name)] = work.tile([P, NQ * CHUNK], F32, name=name)
             return tiles[(c, name)]
 
-        def gate_act(c, gate, q, func, name, lo=0, hi=CHUNK):
+        def gate_act(c, gate, q, func, name):
             d, h = divmod(q, 2)
-            acc = ring_a.tile([P, hi - lo], F32, name="acc", tag="a")
+            acc = ring_a.tile([P, CHUNK], F32, name="acc", tag="a")
             nc.tensor.matmul_mx(
                 out=acc[:],
                 lhsT=w_codes[(gate, d)][:, h * P : (h + 1) * P].bitcast(FP8X4),
                 lhsT_scale=w_scales[(gate, d)][:, h * P : (h + 1) * P],
-                rhs=x_codes[c][:, lo:hi].bitcast(FP8X4),
-                rhs_scale=x_scales[c][:, lo:hi],
+                rhs=x_codes[c][:].bitcast(FP8X4),
+                rhs_scale=x_scales[c][:],
                 start=True,
                 stop=True,
             )
             col = d * 8 + gate * 2 + h
             nc.scalar.activation(
-                out=buf(c, name)[:, q * CHUNK + lo : q * CHUNK + hi],
+                out=buf(c, name)[:, q * CHUNK : (q + 1) * CHUNK],
                 in_=acc[:],
                 func=func,
                 bias=bias[:, col : col + 1],
                 scale=1.0,
             )
 
-        def cell_product(c, q, engine):
+        def cell_product(c, q):
             sl = slice(q * CHUNK, (q + 1) * CHUNK)
-            engine.tensor_tensor(
+            nc.vector.tensor_tensor(
                 out=buf(c, "cell")[:, sl], in0=buf(c, "s_i")[:, sl], in1=buf(c, "t_g")[:, sl], op=ALU.mult
             )
 
@@ -187,33 +175,21 @@ def tile_lstmnetwork_pa_t_kernel(tc, x, w_ih, b_ih, b_hh, out):
                 )
             return bank
 
-        def cell_tanh(c, t, pieces=1):
+        def cell_tanh(c, t):
             bank = turn_back(ring_a, "a", buf(c, "cell"), t)
-            w = 512 // pieces
-            for i in range(pieces):
-                nc.scalar.activation(
-                    out=buf(c, "t_c")[:, t * 512 + i * w : t * 512 + (i + 1) * w],
-                    in_=bank[:, i * w : (i + 1) * w],
-                    func=ACT.Tanh,
-                )
+            nc.scalar.activation(out=buf(c, "t_c")[:, t * 512 : (t + 1) * 512], in_=bank[:], func=ACT.Tanh)
 
-        def hidden(c, t, pieces=1):
+        def hidden(c, t):
             bank = turn_back(ring_v, "v", buf(c, "s_o"), t)
-            w = 512 // pieces
-            for i in range(pieces):
-                sl = slice(t * 512 + i * w, t * 512 + (i + 1) * w)
-                nc.vector.tensor_tensor(
-                    out=buf(c, "hid")[:, sl], in0=bank[:, i * w : (i + 1) * w], in1=buf(c, "t_c")[:, sl], op=ALU.mult
-                )
-                if c == NCHUNK - 1 and t == RT - 1:
-                    nc.sync.dma_start(out=outv[c][:, sl], in_=buf(c, "hid")[:, sl])
+            sl = slice(t * 512, (t + 1) * 512)
+            nc.vector.tensor_tensor(out=buf(c, "hid")[:, sl], in0=bank[:], in1=buf(c, "t_c")[:, sl], op=ALU.mult)
 
         nc.vector.tensor_tensor(out=bsum[0:16, :], in0=bi[:], in1=bh[:], op=ALU.add)
-        turn_x(0, 0, nc.vector.tensor_copy)
-        turn_x(0, 1, nc.vector.tensor_copy)
+        turn_x(0, 0)
+        turn_x(0, 1)
         turn_w(GATE_I, 0, nc.scalar.copy)
         turn_w(GATE_I, 1, nc.scalar.copy)
-        quant_x(0, 0, CHUNK)
+        quant_x(0)
         quant_w(GATE_I, 0)
         bias_ps = ring_v.tile([P, 512], F32, name="bias_ps", tag="v")
         nc.tensor.transpose(bias_ps[:, 0:P], bsum[:], ident[:])
@@ -230,40 +206,25 @@ def tile_lstmnetwork_pa_t_kernel(tc, x, w_ih, b_ih, b_hh, out):
         quant_w(GATE_O, 0)
         quant_w(GATE_O, 1)
 
-        def store(c, t0, t1):
-            nc.sync.dma_start(out=outv[c][:, t0 * 512 : t1 * 512], in_=buf(c, "hid")[:, t0 * 512 : t1 * 512])
-
         for c in range(NCHUNK):
-            last = c == NCHUNK - 1
-            if c > 0:
-                for q in range(NQ):
-                    gate_act(c, GATE_I, q, ACT.Sigmoid, "s_i")
             for q in range(NQ):
                 gate_act(c, GATE_G, q, ACT.Tanh, "t_g")
-            for kind, t in PATTERN:
-                if kind == "c" and c >= 1:
-                    cell_tanh(c - 1, t)
-                if kind == "o" and c >= 2:
-                    hidden(c - 2, t)
-                if kind == "x" and not last:
-                    turn_x(c + 1, t, nc.vector.tensor_copy)
-            if not last:
-                quant_x(c + 1, 0, CHUNK)
-            if c >= 2:
-                store(c - 2, 0, RT)
-            for q in range(NQ):
-                cell_product(c, q, nc.vector)
+                cell_product(c, q)
             for q in range(NQ):
                 gate_act(c, GATE_O, q, ACT.Sigmoid, "s_o")
-        c = NCHUNK - 1
-        for kind, t in TAIL:
-            if kind == "o":
-                hidden(c - 1, t)
-                if t % 2 == 1:
-                    store(c - 1, t - 1, t + 1)
-            else:
-                cell_tanh(c, t, LAST_PIECES if t == RT - 1 else 1)
-        for t in range(RT - 1):
-            hidden(c, t)
-            store(c, t, t + 1)
-        hidden(c, RT - 1, LAST_PIECES)
+            if c + 1 < NCHUNK:
+                turn_x(c + 1, 0)
+                turn_x(c + 1, 1)
+                quant_x(c + 1)
+            for t in range(RT):
+                cell_tanh(c, t)
+            if c + 1 < NCHUNK:
+                for q in range(NQ):
+                    gate_act(c + 1, GATE_I, q, ACT.Sigmoid, "s_i")
+            for t in range(RT):
+                hidden(c, t)
+                if c == NCHUNK - 1:
+                    sl = slice(t * 512, (t + 1) * 512)
+                    nc.sync.dma_start(out=outv[c][:, sl], in_=buf(c, "hid")[:, sl])
+            if c < NCHUNK - 1:
+                nc.sync.dma_start(out=outv[c], in_=buf(c, "hid")[:])

from contextlib import ExitStack

import concourse.masks as masks
import concourse.mybir as mybir

F32 = mybir.dt.float32
BF16 = mybir.dt.bfloat16
U32 = mybir.dt.uint32
U8 = mybir.dt.uint8
FP8X4 = mybir.dt.float8_e4m3fn_x4
ACT = mybir.ActivationFunctionType
ALU = mybir.AluOpType

P = 128
ROWS = 4096
K = 512
H = 256
ND = 2
CHUNK = 512
NCHUNK = ROWS // CHUNK
RT = CHUNK // P
NQ = 4
GATE_I, GATE_G, GATE_O = 0, 2, 3

FLOPS = 2 * ROWS * (3 * H * ND) * K
BYTES = ROWS * K * 2 + ND * 3 * H * K * 2 + 2 * ND * 3 * H * 2 + ROWS * ND * H * 4


def tile_lstmnetwork_pa_t_kernel(tc, x, w_ih, b_ih, b_hh, out):
    nc = tc.nc
    xv = x.flatten_outer_dims().rearrange("(c r t) k -> c r (t k)", r=P, t=RT)
    outv = out.rearrange("(c r t) n -> c r (t n)", r=P, t=RT)

    with ExitStack() as ctx:
        ctx.enter_context(tc.manual_schedule())
        const = ctx.enter_context(tc.tile_pool(name="const", bufs=1))
        xin = ctx.enter_context(tc.tile_pool(name="xin", bufs=1))
        stage = ctx.enter_context(tc.tile_pool(name="stage", bufs=2))
        xq = ctx.enter_context(tc.tile_pool(name="xq", bufs=3))
        work = ctx.enter_context(tc.tile_pool(name="work", bufs=2))
        ring_a = ctx.enter_context(tc.psum_pool(name="ring_a", bufs=5))
        ring_v = ctx.enter_context(tc.psum_pool(name="ring_v", bufs=3))

        bi = const.tile([16, P], BF16, name="bi")
        bh = const.tile([16, P], BF16, name="bh")
        nc.scalar.dma_start(out=bi[:], in_=b_ih.rearrange("d (g p) -> (d g) p", p=P))
        nc.scalar.dma_start(out=bh[:], in_=b_hh.rearrange("d (g p) -> (d g) p", p=P))
        warm = const.tile([P, 1], F32, name="warm")
        nc.vector.memset(warm[:], 0.0)
        nc.scalar.activation(out=warm[:], in_=warm[:], func=ACT.Sigmoid)
        ident = const.tile([P, P], F32, name="ident")
        masks.make_identity(nc, ident[:])
        bsum = const.tile([P, P], F32, name="bsum")
        nc.vector.memset(bsum[:], 0.0)

        w_raw = {}
        x_raw = {}

        def load_w(gate, d):
            t = const.tile([P, 2 * K], BF16, name="wraw%d_%d" % (gate, d))
            nc.sync.dma_start(
                out=t[:].rearrange("p (h k) -> p h k", h=2),
                in_=w_ih[d, gate * H : (gate + 1) * H, :].rearrange("(h p) k -> p h k", p=P),
            )
            w_raw[(gate, d)] = t

        def load_x(c, pieces):
            t = xin.tile([P, RT * K], BF16, name="xraw%d" % c)
            step = RT * K // pieces
            for i in range(pieces):
                nc.sync.dma_start(out=t[:, i * step : (i + 1) * step], in_=xv[c][:, i * step : (i + 1) * step])
            x_raw[c] = t

        load_x(0, 2)
        load_w(GATE_I, 0)
        load_w(GATE_I, 1)
        load_w(GATE_G, 0)
        load_w(GATE_G, 1)
        load_w(GATE_O, 0)
        load_w(GATE_O, 1)
        for c in range(1, NCHUNK):
            load_x(c, 1)

        def turn(raw, first):
            raw32 = raw[:].bitcast(F32)
            bank = ring_v.tile([P, 512], F32, name="turn", tag="v")
            for j in range(2):
                for u in range(2):
                    nc.tensor.transpose(
                        bank[:, (2 * j + u) * P : (2 * j + u + 1) * P],
                        raw32[:, (first + j) * 256 + u * P : (first + j) * 256 + (u + 1) * P],
                        ident[:],
                    )
            return bank

        def regroup(engine_copy, bank, grouped, pair):
            g32 = grouped[:].bitcast(F32)
            engine_copy(
                out=g32[:, pair * 512 : (pair + 1) * 512].rearrange("p (j r u) -> p j r u", j=2, u=2),
                in_=bank[:].rearrange("p (j u r) -> p j r u", j=2, u=2),
            )

        w_grp = {}
        w_codes = {}
        w_scales = {}

        def turn_w(gate, d, engine_copy):
            grouped = stage.tile([P, 4 * 2 * P], BF16, name="wgrp", align_bytes=64, bufs=3)
            regroup(engine_copy, turn(w_raw[(gate, d)], 0), grouped, 0)
            w_grp[(gate, d)] = grouped

        def quant_w(gate, d):
            codes = const.tile([P, 2 * P], U32, name="wc%d_%d" % (gate, d), align_bytes=64)
            scales = const.tile([P, 2 * P], U8, name="ws%d_%d" % (gate, d), align_bytes=64)
            nc.vector.quantize_mx(out=codes[:].bitcast(FP8X4), scales=scales[:], in_=w_grp[(gate, d)][:])
            w_codes[(gate, d)] = codes
            w_scales[(gate, d)] = scales

        x_grp = {}
        x_codes = {}
        x_scales = {}

        def turn_x(c, pair):
            if pair == 0:
                x_grp[c] = stage.tile([P, 4 * CHUNK], BF16, name="xgrp", align_bytes=64)
            regroup(nc.vector.tensor_copy, turn(x_raw[c], 2 * pair), x_grp[c], pair)

        def quant_x(c):
            codes = xq.tile([P, CHUNK], U32, name="xc", align_bytes=64)
            scales = xq.tile([P, CHUNK], U8, name="xs", align_bytes=64)
            nc.vector.quantize_mx(out=codes[:].bitcast(FP8X4), scales=scales[:], in_=x_grp[c][:])
            x_codes[c] = codes
            x_scales[c] = scales

        bias = const.tile([P, 16], F32, name="bias")
        tiles = {}

        def buf(c, name):
            if (c, name) not in tiles:
                tiles[(c, name)] = work.tile([P, NQ * CHUNK], F32, name=name)
            return tiles[(c, name)]

        def gate_act(c, gate, q, func, name):
            d, h = divmod(q, 2)
            acc = ring_a.tile([P, CHUNK], F32, name="acc", tag="a")
            nc.tensor.matmul_mx(
                out=acc[:],
                lhsT=w_codes[(gate, d)][:, h * P : (h + 1) * P].bitcast(FP8X4),
                lhsT_scale=w_scales[(gate, d)][:, h * P : (h + 1) * P],
                rhs=x_codes[c][:].bitcast(FP8X4),
                rhs_scale=x_scales[c][:],
                start=True,
                stop=True,
            )
            col = d * 8 + gate * 2 + h
            nc.scalar.activation(
                out=buf(c, name)[:, q * CHUNK : (q + 1) * CHUNK],
                in_=acc[:],
                func=func,
                bias=bias[:, col : col + 1],
                scale=1.0,
            )

        def cell_product(c, q):
            sl = slice(q * CHUNK, (q + 1) * CHUNK)
            nc.vector.tensor_tensor(
                out=buf(c, "cell")[:, sl], in0=buf(c, "s_i")[:, sl], in1=buf(c, "t_g")[:, sl], op=ALU.mult
            )

        def turn_back(pool, tag, src, t):
            bank = pool.tile([P, 512], F32, name="back_" + tag, tag=tag)
            for q in range(NQ):
                nc.tensor.transpose(
                    bank[:, q * P : (q + 1) * P], src[:, q * CHUNK + t * P : q * CHUNK + (t + 1) * P], ident[:]
                )
            return bank

        def cell_tanh(c, t):
            bank = turn_back(ring_a, "a", buf(c, "cell"), t)
            nc.scalar.activation(out=buf(c, "t_c")[:, t * 512 : (t + 1) * 512], in_=bank[:], func=ACT.Tanh)

        def hidden(c, t):
            bank = turn_back(ring_v, "v", buf(c, "s_o"), t)
            sl = slice(t * 512, (t + 1) * 512)
            nc.vector.tensor_tensor(out=buf(c, "hid")[:, sl], in0=bank[:], in1=buf(c, "t_c")[:, sl], op=ALU.mult)

        nc.vector.tensor_tensor(out=bsum[0:16, :], in0=bi[:], in1=bh[:], op=ALU.add)
        turn_x(0, 0)
        turn_x(0, 1)
        turn_w(GATE_I, 0, nc.scalar.copy)
        turn_w(GATE_I, 1, nc.scalar.copy)
        quant_x(0)
        quant_w(GATE_I, 0)
        bias_ps = ring_v.tile([P, 512], F32, name="bias_ps", tag="v")
        nc.tensor.transpose(bias_ps[:, 0:P], bsum[:], ident[:])
        nc.vector.tensor_copy(out=bias[:], in_=bias_ps[:, 0:16])
        quant_w(GATE_I, 1)
        turn_w(GATE_G, 0, nc.vector.tensor_copy)
        turn_w(GATE_G, 1, nc.vector.tensor_copy)
        for q in range(NQ):
            gate_act(0, GATE_I, q, ACT.Sigmoid, "s_i")
        quant_w(GATE_G, 0)
        quant_w(GATE_G, 1)
        turn_w(GATE_O, 0, nc.vector.tensor_copy)
        turn_w(GATE_O, 1, nc.vector.tensor_copy)
        quant_w(GATE_O, 0)
        quant_w(GATE_O, 1)

        for c in range(NCHUNK):
            for q in range(NQ):
                gate_act(c, GATE_G, q, ACT.Tanh, "t_g")
                cell_product(c, q)
            for q in range(NQ):
                gate_act(c, GATE_O, q, ACT.Sigmoid, "s_o")
            if c + 1 < NCHUNK:
                turn_x(c + 1, 0)
                turn_x(c + 1, 1)
                quant_x(c + 1)
            for t in range(RT):
                cell_tanh(c, t)
            if c + 1 < NCHUNK:
                for q in range(NQ):
                    gate_act(c + 1, GATE_I, q, ACT.Sigmoid, "s_i")
            for t in range(RT):
                hidden(c, t)
                if c == NCHUNK - 1:
                    sl = slice(t * 512, (t + 1) * 512)
                    nc.sync.dma_start(out=outv[c][:, sl], in_=buf(c, "hid")[:, sl])
            if c < NCHUNK - 1:
                nc.sync.dma_start(out=outv[c], in_=buf(c, "hid")[:])
